import numpy as np
import ml_dtypes

BF16 = ml_dtypes.bfloat16


def bf(x):
    return np.asarray(x, np.float32).astype(BF16)


def f32(x):
    return np.asarray(x, np.float32)


def f64(x):
    return np.asarray(x).astype(np.float64)


def striped(idx):
    return np.tile(idx.reshape(-1, 16).T, (8, 1))


C, S, T, H, N = 128, 1024, 6, 512, 6144
SCALE = 1.5


def setup_inputs():
    idx = np.concatenate([np.random.permutation(S)[:H] for _ in range(N // H)])
    return {"z": f32(SCALE * np.random.standard_normal((C, S))), "offs": striped(idx)}


def reference(z, offs):
    idx = offs[:16].T.reshape(-1)
    zz = f64(z)
    e = np.exp(zz)
    q = e / e.sum(0, keepdims=True)
    co = (q[:, idx] * np.tile(q, (1, T))).sum(0)
    pot = -np.log(co).reshape(T, S)
    return pot.sum(0, keepdims=True) - (q * zz).sum(0, keepdims=True)

@@ -1,0 +1,148 @@
+import math
+
+import concourse.mybir as mybir
+from concourse.masks import make_identity
+
+F32 = mybir.dt.float32
+BF16 = mybir.dt.bfloat16
+U16 = mybir.dt.uint16
+ALU = mybir.AluOpType
+ACT = mybir.ActivationFunctionType
+
+P = 128
+NODES = 1024
+NEIGHBOURS = 6
+LIST = NEIGHBOURS * NODES
+BLOCKS = NODES // P
+HALF = 512
+HALF_BLOCKS = HALF // P
+PIECES = LIST // HALF
+
+LN_SHIFT = 62
+
+FLOPS = 2 * P * (LIST + 2 * NODES)
+
+
+def tile_spatialselectivemrf_kernel(tc, z, offs, out):
+    nc = tc.nc
+    with (
+        tc.tile_pool(name="held", bufs=1) as held,
+        tc.tile_pool(name="ring", bufs=3) as ring,
+        tc.psum_pool(name="flipped", bufs=1) as flipped,
+        tc.psum_pool(name="pairs", bufs=2) as pairs,
+        tc.psum_pool(name="total", bufs=1) as total,
+    ):
+        z_sb = held.tile([P, NODES], F32, name="z_sb")
+        offsets = held.tile([P, LIST // 16], U16, name="offsets")
+        nc.sync.dma_start(z_sb[:, 0:HALF], z[:, 0:HALF])
+        nc.scalar.dma_start(z_sb[:, HALF:NODES], z[:, HALF:NODES])
+        nc.sync.dma_start(offsets[:], offs)
+
+        identity = held.tile([P, P], F32, name="identity")
+        make_identity(nc, identity[:])
+        ones = held.tile([P, 1], BF16, name="ones")
+        nc.vector.memset(ones[:], 1.0)
+
+        neg_max = held.tile([P, BLOCKS], F32, name="neg_max")
+        exp_sum = held.tile([P, BLOCKS], F32, name="exp_sum")
+        inv_sum = held.tile([P, BLOCKS], F32, name="inv_sum")
+        score = held.tile([P, BLOCKS], F32, name="score")
+        e_t = held.tile([P, NODES], F32, name="e_t")
+        q_t = held.tile([P, NODES], F32, name="q_t")
+        q_window = held.tile([P, NODES], F32, name="q_window")
+        q_plain = held.tile([P, NODES], F32, name="q_plain")
+
+        z_t = [flipped.tile([P, HALF], F32, name=f"z_t{h}") for h in range(2)]
+        q_ps = [flipped.tile([P, HALF], F32, name=f"q_ps{h}") for h in range(2)]
+
+        for h in range(2):
+            stats = slice(h * HALF_BLOCKS, (h + 1) * HALF_BLOCKS)
+            for b in range(HALF_BLOCKS):
+                block = h * HALF_BLOCKS + b
+                nc.tensor.transpose(z_t[h][:, b * P : (b + 1) * P], z_sb[:, block * P : (block + 1) * P], identity[:])
+            nc.vector.tensor_reduce(
+                out=neg_max[:, stats],
+                in_=z_t[h][:].rearrange("p (b c) -> p b c", c=P),
+                axis=mybir.AxisListType.X,
+                op=ALU.max,
+                negate=True,
+            )
+            for b in range(HALF_BLOCKS):
+                block = h * HALF_BLOCKS + b
+                nc.scalar.activation(
+                    out=e_t[:, block * P : (block + 1) * P],
+                    in_=z_t[h][:, b * P : (b + 1) * P],
+                    func=ACT.Exp,
+                    bias=neg_max[:, block : block + 1],
+                    scale=1.0,
+                    accum_out=exp_sum[:, block : block + 1],
+                )
+
+        for h in range(2):
+            stats = slice(h * HALF_BLOCKS, (h + 1) * HALF_BLOCKS)
+            half = slice(h * HALF, (h + 1) * HALF)
+            nc.vector.reciprocal(inv_sum[:, stats], exp_sum[:, stats])
+            for b in range(HALF_BLOCKS):
+                block = h * HALF_BLOCKS + b
+                nc.vector.tensor_scalar(
+                    out=q_t[:, block * P : (block + 1) * P],
+                    in0=e_t[:, block * P : (block + 1) * P],
+                    scalar1=inv_sum[:, block : block + 1],
+                    scalar2=None,
+                    op0=ALU.mult,
+                )
+                nc.tensor.transpose(q_ps[h][:, b * P : (b + 1) * P], q_t[:, block * P : (block + 1) * P], identity[:])
+            nc.scalar.copy(q_window[:, half], q_ps[h][:])
+            nc.scalar.copy(q_plain[:, half], q_ps[h][:])
+            for b in range(HALF_BLOCKS):
+                block = h * HALF_BLOCKS + b
+                q_z = ring.tile([P, P], F32, name="q_z")
+                nc.vector.scalar_tensor_tensor(
+                    out=q_z[:],
+                    in0=e_t[:, block * P : (block + 1) * P],
+                    scalar=inv_sum[:, block : block + 1],
+                    in1=z_t[h][:, b * P : (b + 1) * P],
+                    op0=ALU.mult,
+                    op1=ALU.mult,
+                    accum_out=score[:, block : block + 1],
+                )
+
+        energy = total.tile([BLOCKS, P], F32, name="energy")
+        nc.tensor.matmul(energy[:], lhsT=score[:], rhs=identity[:], start=True, stop=False)
+
+        for t in range(NEIGHBOURS):
+            co = pairs.tile([P, BLOCKS], F32, name="co")
+            for h in range(2):
+                k = 2 * t + h
+                product = ring.tile([P, HALF], F32, name="product")
+                nc.vector.tensor_tensor(
+                    product[:],
+                    q_window[:].indirect(offsets[:, k * (HALF // 16) : (k + 1) * (HALF // 16)]),
+                    q_plain[:, h * HALF : (h + 1) * HALF],
+                    ALU.mult,
+                )
+                product_bf = ring.tile([P, HALF], BF16, name="product_bf")
+                nc.scalar.copy(product_bf[:], product[:])
+                for b in range(HALF_BLOCKS):
+                    column = h * HALF_BLOCKS + b
+                    nc.tensor.matmul(
+                        co[:, column : column + 1],
+                        lhsT=product_bf[:, b * P : (b + 1) * P],
+                        rhs=ones[:],
+                        start=True,
+                        stop=True,
+                    )
+            log_co = ring.tile([P, BLOCKS], F32, name="log_co")
+            nc.scalar.activation(out=log_co[:], in_=co[:], func=ACT.Ln, scale=2.0**LN_SHIFT)
+            nc.tensor.matmul(energy[:], lhsT=log_co[:], rhs=identity[:], start=False, stop=(t == NEIGHBOURS - 1))
+
+        result = held.tile([BLOCKS, P], F32, name="result")
+        nc.vector.tensor_scalar(
+            out=result[:],
+            in0=energy[:],
+            scalar1=-1.0,
+            scalar2=NEIGHBOURS * LN_SHIFT * math.log(2.0),
+            op0=ALU.mult,
+            op1=ALU.add,
+        )
+        nc.sync.dma_start(out.rearrange("o (b p) -> (o b) p", p=P), result[:])

@@ -108,33 +108,39 @@ def tile_spatialselectivemrf_kernel(tc, z, offs, out):
                 )
 
         energy = total.tile([BLOCKS, P], F32, name="energy")
-        nc.tensor.matmul(energy[:], lhsT=score[:], rhs=identity[:], start=True, stop=False)
+        nc.tensor.matmul(energy[:], lhsT=score[:], rhs=identity[:], start=True, stop=False, is_transpose=True)
 
-        for t in range(NEIGHBOURS):
-            co = pairs.tile([P, BLOCKS], F32, name="co")
-            for h in range(2):
-                k = 2 * t + h
-                product = ring.tile([P, HALF], F32, name="product")
-                nc.vector.tensor_tensor(
-                    product[:],
-                    q_window[:].indirect(offsets[:, k * (HALF // 16) : (k + 1) * (HALF // 16)]),
-                    q_plain[:, h * HALF : (h + 1) * HALF],
-                    ALU.mult,
+        widths = [HALF] * (PIECES - 1) + [P] * HALF_BLOCKS
+        start = 0
+        for width in widths:
+            t, node = divmod(start, NODES)
+            if node == 0:
+                co = pairs.tile([P, BLOCKS], F32, name="co")
+            product = ring.tile([P, HALF], F32, name="product")
+            nc.vector.tensor_tensor(
+                product[:, 0:width],
+                q_window[:].indirect(offsets[:, start // 16 : (start + width) // 16]),
+                q_plain[:, node : node + width],
+                ALU.mult,
+            )
+            product_bf = ring.tile([P, HALF], BF16, name="product_bf")
+            nc.scalar.copy(product_bf[:, 0:width], product[:, 0:width])
+            for b in range(width // P):
+                column = node // P + b
+                nc.tensor.matmul(
+                    co[:, column : column + 1],
+                    lhsT=product_bf[:, b * P : (b + 1) * P],
+                    rhs=ones[:],
+                    start=True,
+                    stop=True,
                 )
-                product_bf = ring.tile([P, HALF], BF16, name="product_bf")
-                nc.scalar.copy(product_bf[:], product[:])
-                for b in range(HALF_BLOCKS):
-                    column = h * HALF_BLOCKS + b
-                    nc.tensor.matmul(
-                        co[:, column : column + 1],
-                        lhsT=product_bf[:, b * P : (b + 1) * P],
-                        rhs=ones[:],
-                        start=True,
-                        stop=True,
-                    )
-            log_co = ring.tile([P, BLOCKS], F32, name="log_co")
-            nc.scalar.activation(out=log_co[:], in_=co[:], func=ACT.Ln, scale=2.0**LN_SHIFT)
-            nc.tensor.matmul(energy[:], lhsT=log_co[:], rhs=identity[:], start=False, stop=(t == NEIGHBOURS - 1))
+            start += width
+            if start % NODES == 0:
+                log_co = ring.tile([P, BLOCKS], F32, name="log_co")
+                nc.scalar.activation(out=log_co[:], in_=co[:], func=ACT.Ln, scale=2.0**LN_SHIFT)
+                nc.tensor.matmul(
+                    energy[:], lhsT=log_co[:], rhs=identity[:], start=False, stop=(start == LIST), is_transpose=True
+                )
 
         result = held.tile([BLOCKS, P], F32, name="result")
         nc.vector.tensor_scalar(

@@ -14,28 +14,35 @@ NODES = 1024
 NEIGHBOURS = 6
 LIST = NEIGHBOURS * NODES
 BLOCKS = NODES // P
+QUARTER = 256
+QUARTERS = NODES // QUARTER
+QUARTER_BLOCKS = QUARTER // P
 HALF = 512
-HALF_BLOCKS = HALF // P
 PIECES = LIST // HALF
+RUN = 8
 
 LN_SHIFT = 62
 
 FLOPS = 2 * P * (LIST + 2 * NODES)
 
 
+def sum_over_clusters(nc, sums, products, ones, first_node):
+    nodes = products.shape[1]
+    by_run = products[:].rearrange("c (m e) -> c e m", e=RUN)
+    rows = slice(first_node // RUN, (first_node + nodes) // RUN)
+    for e in range(RUN):
+        nc.tensor.matmul(sums[rows, e : e + 1], lhsT=by_run[:, e, :], rhs=ones[:], start=True, stop=True)
+
+
 def tile_spatialselectivemrf_kernel(tc, z, offs, out):
     nc = tc.nc
-    with (
-        tc.tile_pool(name="held", bufs=1) as held,
-        tc.tile_pool(name="ring", bufs=3) as ring,
-        tc.psum_pool(name="flipped", bufs=1) as flipped,
-        tc.psum_pool(name="pairs", bufs=2) as pairs,
-        tc.psum_pool(name="total", bufs=1) as total,
-    ):
+    with tc.tile_pool(name="held", bufs=1) as held, tc.tile_pool(name="ring", bufs=3) as ring:
         z_sb = held.tile([P, NODES], F32, name="z_sb")
         offsets = held.tile([P, LIST // 16], U16, name="offsets")
-        nc.sync.dma_start(z_sb[:, 0:HALF], z[:, 0:HALF])
-        nc.scalar.dma_start(z_sb[:, HALF:NODES], z[:, HALF:NODES])
+        for g in range(QUARTERS):
+            quarter = slice(g * QUARTER, (g + 1) * QUARTER)
+            queue = nc.sync if g % 2 == 0 else nc.scalar
+            queue.dma_start(z_sb[:, quarter], z[:, quarter])
         nc.sync.dma_start(offsets[:], offs)
 
         identity = held.tile([P, P], F32, name="identity")
@@ -46,109 +53,95 @@ def tile_spatialselectivemrf_kernel(tc, z, offs, out):
         neg_max = held.tile([P, BLOCKS], F32, name="neg_max")
         exp_sum = held.tile([P, BLOCKS], F32, name="exp_sum")
         inv_sum = held.tile([P, BLOCKS], F32, name="inv_sum")
-        score = held.tile([P, BLOCKS], F32, name="score")
         e_t = held.tile([P, NODES], F32, name="e_t")
         q_t = held.tile([P, NODES], F32, name="q_t")
         q_window = held.tile([P, NODES], F32, name="q_window")
         q_plain = held.tile([P, NODES], F32, name="q_plain")
 
-        z_t = [flipped.tile([P, HALF], F32, name=f"z_t{h}") for h in range(2)]
-        q_ps = [flipped.tile([P, HALF], F32, name=f"q_ps{h}") for h in range(2)]
+        with tc.psum_pool(name="flipped", bufs=1) as flipped:
+            z_t = [flipped.tile([P, QUARTER], F32, name=f"z_t{g}") for g in range(QUARTERS)]
+            q_ps = [flipped.tile([P, QUARTER], F32, name=f"q_ps{g}") for g in range(QUARTERS)]
 
-        for h in range(2):
-            stats = slice(h * HALF_BLOCKS, (h + 1) * HALF_BLOCKS)
-            for b in range(HALF_BLOCKS):
-                block = h * HALF_BLOCKS + b
-                nc.tensor.transpose(z_t[h][:, b * P : (b + 1) * P], z_sb[:, block * P : (block + 1) * P], identity[:])
+            for g in range(QUARTERS):
+                stats = slice(g * QUARTER_BLOCKS, (g + 1) * QUARTER_BLOCKS)
+                for b in range(QUARTER_BLOCKS):
+                    block = g * QUARTER_BLOCKS + b
+                    nc.tensor.transpose(z_t[g][:, b * P : (b + 1) * P], z_sb[:, block * P : (block + 1) * P], identity[:])
+                nc.vector.tensor_reduce(
+                    out=neg_max[:, stats],
+                    in_=z_t[g][:].rearrange("p (b c) -> p b c", c=P),
+                    axis=mybir.AxisListType.X,
+                    op=ALU.max,
+                    negate=True,
+                )
+                for b in range(QUARTER_BLOCKS):
+                    block = g * QUARTER_BLOCKS + b
+                    nc.scalar.activation(
+                        out=e_t[:, block * P : (block + 1) * P],
+                        in_=z_t[g][:, b * P : (b + 1) * P],
+                        func=ACT.Exp,
+                        bias=neg_max[:, block : block + 1],
+                        scale=1.0,
+                        accum_out=exp_sum[:, block : block + 1],
+                    )
+
+            for g in range(QUARTERS):
+                stats = slice(g * QUARTER_BLOCKS, (g + 1) * QUARTER_BLOCKS)
+                quarter = slice(g * QUARTER, (g + 1) * QUARTER)
+                nc.vector.reciprocal(inv_sum[:, stats], exp_sum[:, stats])
+                for b in range(QUARTER_BLOCKS):
+                    block = g * QUARTER_BLOCKS + b
+                    nc.vector.tensor_scalar(
+                        out=q_t[:, block * P : (block + 1) * P],
+                        in0=e_t[:, block * P : (block + 1) * P],
+                        scalar1=inv_sum[:, block : block + 1],
+                        scalar2=None,
+                        op0=ALU.mult,
+                    )
+                    nc.tensor.transpose(q_ps[g][:, b * P : (b + 1) * P], q_t[:, block * P : (block + 1) * P], identity[:])
+                nc.scalar.copy(q_window[:, quarter], q_ps[g][:])
+
+        with tc.psum_pool(name="pairs", bufs=2) as pairs, tc.psum_pool(name="total", bufs=1) as total:
+            score_ps = total.tile([P, RUN], F32, name="score_ps")
+            for g in range(QUARTERS):
+                quarter = slice(g * QUARTER, (g + 1) * QUARTER)
+                q_z = ring.tile([P, QUARTER], BF16, name="q_z")
+                nc.vector.tensor_tensor(q_z[:], q_window[:, quarter], z_sb[:, quarter], ALU.mult)
+                sum_over_clusters(nc, score_ps, q_z, ones, g * QUARTER)
+                if g == 1:
+                    nc.vector.tensor_copy(q_plain[:, 0:HALF], q_window[:, 0:HALF])
+            nc.scalar.copy(q_plain[:, HALF:NODES], q_window[:, HALF:NODES])
+
+            terms = held.tile([P, (NEIGHBOURS + 1) * RUN], F32, name="terms")
+            nc.scalar.activation(
+                out=terms[:, NEIGHBOURS * RUN : (NEIGHBOURS + 1) * RUN],
+                in_=score_ps[:],
+                func=ACT.Copy,
+                bias=-NEIGHBOURS * LN_SHIFT * math.log(2.0),
+            )
+
+            for t in range(NEIGHBOURS):
+                co = pairs.tile([P, RUN], F32, name="co")
+                for h in range(2):
+                    k = 2 * t + h
+                    product = ring.tile([P, HALF], F32, name="product")
+                    nc.vector.tensor_tensor(
+                        product[:],
+                        q_window[:].indirect(offsets[:, k * (HALF // 16) : (k + 1) * (HALF // 16)]),
+                        q_plain[:, h * HALF : (h + 1) * HALF],
+                        ALU.mult,
+                    )
+                    product_bf = ring.tile([P, HALF], BF16, name="product_bf")
+                    nc.scalar.copy(product_bf[:], product[:])
+                    sum_over_clusters(nc, co, product_bf, ones, h * HALF)
+                nc.scalar.activation(out=terms[:, t * RUN : (t + 1) * RUN], in_=co[:], func=ACT.Ln, scale=2.0**LN_SHIFT)
+
+            result = held.tile([P, RUN], F32, name="result")
             nc.vector.tensor_reduce(
-                out=neg_max[:, stats],
-                in_=z_t[h][:].rearrange("p (b c) -> p b c", c=P),
+                out=result[:],
+                in_=terms[:].rearrange("p (t e) -> p e t", e=RUN),
                 axis=mybir.AxisListType.X,
-                op=ALU.max,
+                op=ALU.add,
                 negate=True,
             )
-            for b in range(HALF_BLOCKS):
-                block = h * HALF_BLOCKS + b
-                nc.scalar.activation(
-                    out=e_t[:, block * P : (block + 1) * P],
-                    in_=z_t[h][:, b * P : (b + 1) * P],
-                    func=ACT.Exp,
-                    bias=neg_max[:, block : block + 1],
-                    scale=1.0,
-                    accum_out=exp_sum[:, block : block + 1],
-                )
-
-        for h in range(2):
-            stats = slice(h * HALF_BLOCKS, (h + 1) * HALF_BLOCKS)
-            half = slice(h * HALF, (h + 1) * HALF)
-            nc.vector.reciprocal(inv_sum[:, stats], exp_sum[:, stats])
-            for b in range(HALF_BLOCKS):
-                block = h * HALF_BLOCKS + b
-                nc.vector.tensor_scalar(
-                    out=q_t[:, block * P : (block + 1) * P],
-                    in0=e_t[:, block * P : (block + 1) * P],
-                    scalar1=inv_sum[:, block : block + 1],
-                    scalar2=None,
-                    op0=ALU.mult,
-                )
-                nc.tensor.transpose(q_ps[h][:, b * P : (b + 1) * P], q_t[:, block * P : (block + 1) * P], identity[:])
-            nc.scalar.copy(q_window[:, half], q_ps[h][:])
-            nc.scalar.copy(q_plain[:, half], q_ps[h][:])
-            for b in range(HALF_BLOCKS):
-                block = h * HALF_BLOCKS + b
-                q_z = ring.tile([P, P], F32, name="q_z")
-                nc.vector.scalar_tensor_tensor(
-                    out=q_z[:],
-                    in0=e_t[:, block * P : (block + 1) * P],
-                    scalar=inv_sum[:, block : block + 1],
-                    in1=z_t[h][:, b * P : (b + 1) * P],
-                    op0=ALU.mult,
-                    op1=ALU.mult,
-                    accum_out=score[:, block : block + 1],
-                )
-
-        energy = total.tile([BLOCKS, P], F32, name="energy")
-        nc.tensor.matmul(energy[:], lhsT=score[:], rhs=identity[:], start=True, stop=False, is_transpose=True)
-
-        widths = [HALF] * (PIECES - 1) + [P] * HALF_BLOCKS
-        start = 0
-        for width in widths:
-            t, node = divmod(start, NODES)
-            if node == 0:
-                co = pairs.tile([P, BLOCKS], F32, name="co")
-            product = ring.tile([P, HALF], F32, name="product")
-            nc.vector.tensor_tensor(
-                product[:, 0:width],
-                q_window[:].indirect(offsets[:, start // 16 : (start + width) // 16]),
-                q_plain[:, node : node + width],
-                ALU.mult,
-            )
-            product_bf = ring.tile([P, HALF], BF16, name="product_bf")
-            nc.scalar.copy(product_bf[:, 0:width], product[:, 0:width])
-            for b in range(width // P):
-                column = node // P + b
-                nc.tensor.matmul(
-                    co[:, column : column + 1],
-                    lhsT=product_bf[:, b * P : (b + 1) * P],
-                    rhs=ones[:],
-                    start=True,
-                    stop=True,
-                )
-            start += width
-            if start % NODES == 0:
-                log_co = ring.tile([P, BLOCKS], F32, name="log_co")
-                nc.scalar.activation(out=log_co[:], in_=co[:], func=ACT.Ln, scale=2.0**LN_SHIFT)
-                nc.tensor.matmul(
-                    energy[:], lhsT=log_co[:], rhs=identity[:], start=False, stop=(start == LIST), is_transpose=True
-                )
-
-        result = held.tile([BLOCKS, P], F32, name="result")
-        nc.vector.tensor_scalar(
-            out=result[:],
-            in0=energy[:],
-            scalar1=-1.0,
-            scalar2=NEIGHBOURS * LN_SHIFT * math.log(2.0),
-            op0=ALU.mult,
-            op1=ALU.add,
-        )
-        nc.sync.dma_start(out.rearrange("o (b p) -> (o b) p", p=P), result[:])
+            nc.sync.dma_start(out.rearrange("o (p e) -> (o p) e", e=RUN), result[:])

@@ -34,6 +34,13 @@ def sum_over_clusters(nc, sums, products, ones, first_node):
         nc.tensor.matmul(sums[rows, e : e + 1], lhsT=by_run[:, e, :], rhs=ones[:], start=True, stop=True)
 
 
+def score_of_quarter(nc, ring, score, q, z_sb, ones, g):
+    quarter = slice(g * QUARTER, (g + 1) * QUARTER)
+    q_z = ring.tile([P, QUARTER], BF16, name="q_z")
+    nc.vector.tensor_tensor(q_z[:], q[:, quarter], z_sb[:, quarter], ALU.mult)
+    sum_over_clusters(nc, score, q_z, ones, g * QUARTER)
+
+
 def tile_spatialselectivemrf_kernel(tc, z, offs, out):
     nc = tc.nc
     with tc.tile_pool(name="held", bufs=1) as held, tc.tile_pool(name="ring", bufs=3) as ring:
@@ -102,24 +109,14 @@ def tile_spatialselectivemrf_kernel(tc, z, offs, out):
                 nc.scalar.copy(q_window[:, quarter], q_ps[g][:])
 
         with tc.psum_pool(name="pairs", bufs=2) as pairs, tc.psum_pool(name="total", bufs=1) as total:
-            score_ps = total.tile([P, RUN], F32, name="score_ps")
-            for g in range(QUARTERS):
-                quarter = slice(g * QUARTER, (g + 1) * QUARTER)
-                q_z = ring.tile([P, QUARTER], BF16, name="q_z")
-                nc.vector.tensor_tensor(q_z[:], q_window[:, quarter], z_sb[:, quarter], ALU.mult)
-                sum_over_clusters(nc, score_ps, q_z, ones, g * QUARTER)
-                if g == 1:
-                    nc.vector.tensor_copy(q_plain[:, 0:HALF], q_window[:, 0:HALF])
+            score = total.tile([P, RUN], F32, name="score")
+            for g in range(QUARTERS // 2):
+                score_of_quarter(nc, ring, score, q_window, z_sb, ones, g)
+
+            nc.vector.tensor_copy(q_plain[:, 0:HALF], q_window[:, 0:HALF])
             nc.scalar.copy(q_plain[:, HALF:NODES], q_window[:, HALF:NODES])
 
             terms = held.tile([P, (NEIGHBOURS + 1) * RUN], F32, name="terms")
-            nc.scalar.activation(
-                out=terms[:, NEIGHBOURS * RUN : (NEIGHBOURS + 1) * RUN],
-                in_=score_ps[:],
-                func=ACT.Copy,
-                bias=-NEIGHBOURS * LN_SHIFT * math.log(2.0),
-            )
-
             for t in range(NEIGHBOURS):
                 co = pairs.tile([P, RUN], F32, name="co")
                 for h in range(2):
@@ -132,9 +129,19 @@ def tile_spatialselectivemrf_kernel(tc, z, offs, out):
                         ALU.mult,
                     )
                     product_bf = ring.tile([P, HALF], BF16, name="product_bf")
-                    nc.scalar.copy(product_bf[:], product[:])
+                    if k < PIECES - 1:
+                        nc.scalar.copy(product_bf[:], product[:])
+                    else:
+                        nc.vector.tensor_copy(product_bf[:], product[:])
                     sum_over_clusters(nc, co, product_bf, ones, h * HALF)
                 nc.scalar.activation(out=terms[:, t * RUN : (t + 1) * RUN], in_=co[:], func=ACT.Ln, scale=2.0**LN_SHIFT)
+
+            for g in range(QUARTERS // 2, QUARTERS):
+                score_of_quarter(nc, ring, score, q_window, z_sb, ones, g)
+
+            nc.vector.tensor_scalar_add(
+                terms[:, NEIGHBOURS * RUN : (NEIGHBOURS + 1) * RUN], score[:], -NEIGHBOURS * LN_SHIFT * math.log(2.0)
+            )
 
             result = held.tile([P, RUN], F32, name="result")
             nc.vector.tensor_reduce(

@@ -18,7 +18,7 @@ QUARTER = 256
 QUARTERS = NODES // QUARTER
 QUARTER_BLOCKS = QUARTER // P
 HALF = 512
-PIECES = LIST // HALF
+HALVES = NODES // HALF
 RUN = 8
 
 LN_SHIFT = 62
@@ -28,17 +28,10 @@ FLOPS = 2 * P * (LIST + 2 * NODES)
 
 def sum_over_clusters(nc, sums, products, ones, first_node):
     nodes = products.shape[1]
-    by_run = products[:].rearrange("c (m e) -> c e m", e=RUN)
+    by_run = products[:].rearrange("c (m r) -> c r m", r=RUN)
     rows = slice(first_node // RUN, (first_node + nodes) // RUN)
-    for e in range(RUN):
-        nc.tensor.matmul(sums[rows, e : e + 1], lhsT=by_run[:, e, :], rhs=ones[:], start=True, stop=True)
-
-
-def score_of_quarter(nc, ring, score, q, z_sb, ones, g):
-    quarter = slice(g * QUARTER, (g + 1) * QUARTER)
-    q_z = ring.tile([P, QUARTER], BF16, name="q_z")
-    nc.vector.tensor_tensor(q_z[:], q[:, quarter], z_sb[:, quarter], ALU.mult)
-    sum_over_clusters(nc, score, q_z, ones, g * QUARTER)
+    for r in range(RUN):
+        nc.tensor.matmul(sums[rows, r : r + 1], lhsT=by_run[:, r, :], rhs=ones[:], start=True, stop=True)
 
 
 def tile_spatialselectivemrf_kernel(tc, z, offs, out):
@@ -46,10 +39,9 @@ def tile_spatialselectivemrf_kernel(tc, z, offs, out):
     with tc.tile_pool(name="held", bufs=1) as held, tc.tile_pool(name="ring", bufs=3) as ring:
         z_sb = held.tile([P, NODES], F32, name="z_sb")
         offsets = held.tile([P, LIST // 16], U16, name="offsets")
-        for g in range(QUARTERS):
-            quarter = slice(g * QUARTER, (g + 1) * QUARTER)
-            queue = nc.sync if g % 2 == 0 else nc.scalar
-            queue.dma_start(z_sb[:, quarter], z[:, quarter])
+        for block in range(BLOCKS):
+            queue = nc.sync if block % 2 == 0 else nc.scalar
+            queue.dma_start(z_sb[:, block * P : (block + 1) * P], z[:, block * P : (block + 1) * P])
         nc.sync.dma_start(offsets[:], offs)
 
         identity = held.tile([P, P], F32, name="identity")
@@ -109,18 +101,28 @@ def tile_spatialselectivemrf_kernel(tc, z, offs, out):
                 nc.scalar.copy(q_window[:, quarter], q_ps[g][:])
 
         with tc.psum_pool(name="pairs", bufs=2) as pairs, tc.psum_pool(name="total", bufs=1) as total:
-            score = total.tile([P, RUN], F32, name="score")
-            for g in range(QUARTERS // 2):
-                score_of_quarter(nc, ring, score, q_window, z_sb, ones, g)
-
-            nc.vector.tensor_copy(q_plain[:, 0:HALF], q_window[:, 0:HALF])
+            score_ps = total.tile([P, RUN], F32, name="score_ps")
+            for g in range(QUARTERS):
+                quarter = slice(g * QUARTER, (g + 1) * QUARTER)
+                q_z = ring.tile([P, QUARTER], BF16, name="q_z")
+                nc.vector.tensor_tensor(q_z[:], q_window[:, quarter], z_sb[:, quarter], ALU.mult)
+                sum_over_clusters(nc, score_ps, q_z, ones, g * QUARTER)
+                if (g + 1) * QUARTER == HALF:
+                    nc.vector.tensor_copy(q_plain[:, 0:HALF], q_window[:, 0:HALF])
             nc.scalar.copy(q_plain[:, HALF:NODES], q_window[:, HALF:NODES])
 
             terms = held.tile([P, (NEIGHBOURS + 1) * RUN], F32, name="terms")
+            nc.scalar.activation(
+                out=terms[:, NEIGHBOURS * RUN : (NEIGHBOURS + 1) * RUN],
+                in_=score_ps[:],
+                func=ACT.Copy,
+                bias=-NEIGHBOURS * LN_SHIFT * math.log(2.0),
+            )
+
             for t in range(NEIGHBOURS):
                 co = pairs.tile([P, RUN], F32, name="co")
-                for h in range(2):
-                    k = 2 * t + h
+                for h in range(HALVES):
+                    k = HALVES * t + h
                     product = ring.tile([P, HALF], F32, name="product")
                     nc.vector.tensor_tensor(
                         product[:],
@@ -129,26 +131,16 @@ def tile_spatialselectivemrf_kernel(tc, z, offs, out):
                         ALU.mult,
                     )
                     product_bf = ring.tile([P, HALF], BF16, name="product_bf")
-                    if k < PIECES - 1:
-                        nc.scalar.copy(product_bf[:], product[:])
-                    else:
-                        nc.vector.tensor_copy(product_bf[:], product[:])
+                    nc.scalar.copy(product_bf[:], product[:])
                     sum_over_clusters(nc, co, product_bf, ones, h * HALF)
                 nc.scalar.activation(out=terms[:, t * RUN : (t + 1) * RUN], in_=co[:], func=ACT.Ln, scale=2.0**LN_SHIFT)
-
-            for g in range(QUARTERS // 2, QUARTERS):
-                score_of_quarter(nc, ring, score, q_window, z_sb, ones, g)
-
-            nc.vector.tensor_scalar_add(
-                terms[:, NEIGHBOURS * RUN : (NEIGHBOURS + 1) * RUN], score[:], -NEIGHBOURS * LN_SHIFT * math.log(2.0)
-            )
 
             result = held.tile([P, RUN], F32, name="result")
             nc.vector.tensor_reduce(
                 out=result[:],
-                in_=terms[:].rearrange("p (t e) -> p e t", e=RUN),
+                in_=terms[:].rearrange("p (t r) -> p r t", r=RUN),
                 axis=mybir.AxisListType.X,
                 op=ALU.add,
                 negate=True,
             )
-            nc.sync.dma_start(out.rearrange("o (p e) -> (o p) e", e=RUN), result[:])
+            nc.sync.dma_start(out.rearrange("o (p r) -> (o p) r", r=RUN), result[:])

@@ -40,8 +40,7 @@ def tile_spatialselectivemrf_kernel(tc, z, offs, out):
         z_sb = held.tile([P, NODES], F32, name="z_sb")
         offsets = held.tile([P, LIST // 16], U16, name="offsets")
         for block in range(BLOCKS):
-            queue = nc.sync if block % 2 == 0 else nc.scalar
-            queue.dma_start(z_sb[:, block * P : (block + 1) * P], z[:, block * P : (block + 1) * P])
+            nc.sync.dma_start(z_sb[:, block * P : (block + 1) * P], z[:, block * P : (block + 1) * P])
         nc.sync.dma_start(offsets[:], offs)
 
         identity = held.tile([P, P], F32, name="identity")

@@ -39,8 +39,9 @@ def tile_spatialselectivemrf_kernel(tc, z, offs, out):
     with tc.tile_pool(name="held", bufs=1) as held, tc.tile_pool(name="ring", bufs=3) as ring:
         z_sb = held.tile([P, NODES], F32, name="z_sb")
         offsets = held.tile([P, LIST // 16], U16, name="offsets")
-        for block in range(BLOCKS):
-            nc.sync.dma_start(z_sb[:, block * P : (block + 1) * P], z[:, block * P : (block + 1) * P])
+        for g in range(QUARTERS):
+            quarter = slice(g * QUARTER, (g + 1) * QUARTER)
+            nc.sync.dma_start(z_sb[:, quarter], z[:, quarter])
         nc.sync.dma_start(offsets[:], offs)
 
         identity = held.tile([P, P], F32, name="identity")

@@ -17,8 +17,7 @@ BLOCKS = NODES // P
 QUARTER = 256
 QUARTERS = NODES // QUARTER
 QUARTER_BLOCKS = QUARTER // P
-HALF = 512
-HALVES = NODES // HALF
+HALF = NODES // 2
 RUN = 8
 
 LN_SHIFT = 62
@@ -26,12 +25,10 @@ LN_SHIFT = 62
 FLOPS = 2 * P * (LIST + 2 * NODES)
 
 
-def sum_over_clusters(nc, sums, products, ones, first_node):
-    nodes = products.shape[1]
-    by_run = products[:].rearrange("c (m r) -> c r m", r=RUN)
-    rows = slice(first_node // RUN, (first_node + nodes) // RUN)
+def sum_over_clusters(nc, sums, products, ones):
+    by_run = products[:].rearrange("c (p r) -> c r p", r=RUN)
     for r in range(RUN):
-        nc.tensor.matmul(sums[rows, r : r + 1], lhsT=by_run[:, r, :], rhs=ones[:], start=True, stop=True)
+        nc.tensor.matmul(sums[:, r : r + 1], lhsT=by_run[:, r, :], rhs=ones[:], start=True, stop=True)
 
 
 def tile_spatialselectivemrf_kernel(tc, z, offs, out):
@@ -102,14 +99,12 @@ def tile_spatialselectivemrf_kernel(tc, z, offs, out):
 
         with tc.psum_pool(name="pairs", bufs=2) as pairs, tc.psum_pool(name="total", bufs=1) as total:
             score_ps = total.tile([P, RUN], F32, name="score_ps")
+            q_z = held.tile([P, NODES], BF16, name="q_z")
             for g in range(QUARTERS):
                 quarter = slice(g * QUARTER, (g + 1) * QUARTER)
-                q_z = ring.tile([P, QUARTER], BF16, name="q_z")
-                nc.vector.tensor_tensor(q_z[:], q_window[:, quarter], z_sb[:, quarter], ALU.mult)
-                sum_over_clusters(nc, score_ps, q_z, ones, g * QUARTER)
-                if (g + 1) * QUARTER == HALF:
-                    nc.vector.tensor_copy(q_plain[:, 0:HALF], q_window[:, 0:HALF])
-            nc.scalar.copy(q_plain[:, HALF:NODES], q_window[:, HALF:NODES])
+                nc.vector.tensor_copy(q_plain[:, quarter], q_window[:, quarter])
+                nc.vector.tensor_tensor(q_z[:, quarter], q_window[:, quarter], z_sb[:, quarter], ALU.mult)
+            sum_over_clusters(nc, score_ps, q_z, ones)
 
             terms = held.tile([P, (NEIGHBOURS + 1) * RUN], F32, name="terms")
             nc.scalar.activation(
@@ -120,19 +115,21 @@ def tile_spatialselectivemrf_kernel(tc, z, offs, out):
             )
 
             for t in range(NEIGHBOURS):
-                co = pairs.tile([P, RUN], F32, name="co")
-                for h in range(HALVES):
-                    k = HALVES * t + h
-                    product = ring.tile([P, HALF], F32, name="product")
-                    nc.vector.tensor_tensor(
-                        product[:],
-                        q_window[:].indirect(offsets[:, k * (HALF // 16) : (k + 1) * (HALF // 16)]),
-                        q_plain[:, h * HALF : (h + 1) * HALF],
-                        ALU.mult,
-                    )
-                    product_bf = ring.tile([P, HALF], BF16, name="product_bf")
+                product = ring.tile([P, NODES], F32, name="product")
+                nc.vector.tensor_tensor(
+                    product[:],
+                    q_window[:].indirect(offsets[:, t * (NODES // 16) : (t + 1) * (NODES // 16)]),
+                    q_plain[:],
+                    ALU.mult,
+                )
+                product_bf = ring.tile([P, NODES], BF16, name="product_bf")
+                if t < NEIGHBOURS - 1:
                     nc.scalar.copy(product_bf[:], product[:])
-                    sum_over_clusters(nc, co, product_bf, ones, h * HALF)
+                else:
+                    nc.scalar.copy(product_bf[:, 0:HALF], product[:, 0:HALF])
+                    nc.vector.tensor_copy(product_bf[:, HALF:NODES], product[:, HALF:NODES])
+                co = pairs.tile([P, RUN], F32, name="co")
+                sum_over_clusters(nc, co, product_bf, ones)
                 nc.scalar.activation(out=terms[:, t * RUN : (t + 1) * RUN], in_=co[:], func=ACT.Ln, scale=2.0**LN_SHIFT)
 
             result = held.tile([P, RUN], F32, name="result")

@@ -25,10 +25,12 @@ LN_SHIFT = 62
 FLOPS = 2 * P * (LIST + 2 * NODES)
 
 
-def sum_over_clusters(nc, sums, products, ones):
-    by_run = products[:].rearrange("c (p r) -> c r p", r=RUN)
+def sum_over_clusters(nc, sums, products, ones, first_node):
+    nodes = products.shape[1]
+    by_run = products.rearrange("c (m r) -> c r m", r=RUN)
+    rows = slice(first_node // RUN, (first_node + nodes) // RUN)
     for r in range(RUN):
-        nc.tensor.matmul(sums[:, r : r + 1], lhsT=by_run[:, r, :], rhs=ones[:], start=True, stop=True)
+        nc.tensor.matmul(sums[rows, r : r + 1], lhsT=by_run[:, r, :], rhs=ones[:], start=True, stop=True)
 
 
 def tile_spatialselectivemrf_kernel(tc, z, offs, out):
@@ -82,9 +84,10 @@ def tile_spatialselectivemrf_kernel(tc, z, offs, out):
                     )
 
             for g in range(QUARTERS):
-                stats = slice(g * QUARTER_BLOCKS, (g + 1) * QUARTER_BLOCKS)
                 quarter = slice(g * QUARTER, (g + 1) * QUARTER)
-                nc.vector.reciprocal(inv_sum[:, stats], exp_sum[:, stats])
+                if g % 2 == 0:
+                    stats = slice(g * QUARTER_BLOCKS, (g + 2) * QUARTER_BLOCKS)
+                    nc.vector.reciprocal(inv_sum[:, stats], exp_sum[:, stats])
                 for b in range(QUARTER_BLOCKS):
                     block = g * QUARTER_BLOCKS + b
                     nc.vector.tensor_scalar(
@@ -102,9 +105,11 @@ def tile_spatialselectivemrf_kernel(tc, z, offs, out):
             q_z = held.tile([P, NODES], BF16, name="q_z")
             for g in range(QUARTERS):
                 quarter = slice(g * QUARTER, (g + 1) * QUARTER)
-                nc.vector.tensor_copy(q_plain[:, quarter], q_window[:, quarter])
                 nc.vector.tensor_tensor(q_z[:, quarter], q_window[:, quarter], z_sb[:, quarter], ALU.mult)
-            sum_over_clusters(nc, score_ps, q_z, ones)
+                if (g + 1) * QUARTER == HALF:
+                    nc.vector.tensor_copy(q_plain[:, 0:HALF], q_window[:, 0:HALF])
+            nc.scalar.copy(q_plain[:, HALF:NODES], q_window[:, HALF:NODES])
+            sum_over_clusters(nc, score_ps, q_z[:], ones, 0)
 
             terms = held.tile([P, (NEIGHBOURS + 1) * RUN], F32, name="terms")
             nc.scalar.activation(
@@ -115,21 +120,24 @@ def tile_spatialselectivemrf_kernel(tc, z, offs, out):
             )
 
             for t in range(NEIGHBOURS):
-                product = ring.tile([P, NODES], F32, name="product")
-                nc.vector.tensor_tensor(
-                    product[:],
-                    q_window[:].indirect(offsets[:, t * (NODES // 16) : (t + 1) * (NODES // 16)]),
-                    q_plain[:],
-                    ALU.mult,
-                )
-                product_bf = ring.tile([P, NODES], BF16, name="product_bf")
-                if t < NEIGHBOURS - 1:
-                    nc.scalar.copy(product_bf[:], product[:])
-                else:
-                    nc.scalar.copy(product_bf[:, 0:HALF], product[:, 0:HALF])
-                    nc.vector.tensor_copy(product_bf[:, HALF:NODES], product[:, HALF:NODES])
                 co = pairs.tile([P, RUN], F32, name="co")
-                sum_over_clusters(nc, co, product_bf, ones)
+                nodes = HALF if t == 0 else NODES
+                for first_node in range(0, NODES, nodes):
+                    first_column = (t * NODES + first_node) // 16
+                    product = ring.tile([P, nodes], F32, name="product", tag=f"product{nodes}")
+                    nc.vector.tensor_tensor(
+                        product[:],
+                        q_window[:].indirect(offsets[:, first_column : first_column + nodes // 16]),
+                        q_plain[:, first_node : first_node + nodes],
+                        ALU.mult,
+                    )
+                    product_bf = ring.tile([P, nodes], BF16, name="product_bf", tag=f"product_bf{nodes}")
+                    if t < NEIGHBOURS - 1:
+                        nc.scalar.copy(product_bf[:], product[:])
+                    else:
+                        nc.scalar.copy(product_bf[:, 0:HALF], product[:, 0:HALF])
+                        nc.vector.tensor_copy(product_bf[:, HALF:NODES], product[:, HALF:NODES])
+                    sum_over_clusters(nc, co, product_bf[:], ones, first_node)
                 nc.scalar.activation(out=terms[:, t * RUN : (t + 1) * RUN], in_=co[:], func=ACT.Ln, scale=2.0**LN_SHIFT)
 
             result = held.tile([P, RUN], F32, name="result")

@@ -25,12 +25,10 @@ LN_SHIFT = 62
 FLOPS = 2 * P * (LIST + 2 * NODES)
 
 
-def sum_over_clusters(nc, sums, products, ones, first_node):
-    nodes = products.shape[1]
-    by_run = products.rearrange("c (m r) -> c r m", r=RUN)
-    rows = slice(first_node // RUN, (first_node + nodes) // RUN)
+def sum_over_clusters(nc, sums, products, ones):
+    by_run = products[:].rearrange("c (p r) -> c r p", r=RUN)
     for r in range(RUN):
-        nc.tensor.matmul(sums[rows, r : r + 1], lhsT=by_run[:, r, :], rhs=ones[:], start=True, stop=True)
+        nc.tensor.matmul(sums[:, r : r + 1], lhsT=by_run[:, r, :], rhs=ones[:], start=True, stop=True)
 
 
 def tile_spatialselectivemrf_kernel(tc, z, offs, out):
@@ -109,7 +107,7 @@ def tile_spatialselectivemrf_kernel(tc, z, offs, out):
                 if (g + 1) * QUARTER == HALF:
                     nc.vector.tensor_copy(q_plain[:, 0:HALF], q_window[:, 0:HALF])
             nc.scalar.copy(q_plain[:, HALF:NODES], q_window[:, HALF:NODES])
-            sum_over_clusters(nc, score_ps, q_z[:], ones, 0)
+            sum_over_clusters(nc, score_ps, q_z, ones)
 
             terms = held.tile([P, (NEIGHBOURS + 1) * RUN], F32, name="terms")
             nc.scalar.activation(
@@ -120,24 +118,24 @@ def tile_spatialselectivemrf_kernel(tc, z, offs, out):
             )
 
             for t in range(NEIGHBOURS):
-                co = pairs.tile([P, RUN], F32, name="co")
-                nodes = HALF if t == 0 else NODES
+                product = ring.tile([P, NODES], F32, name="product")
+                product_bf = ring.tile([P, NODES], BF16, name="product_bf")
+                nodes = HALF if t in (0, NEIGHBOURS - 1) else NODES
                 for first_node in range(0, NODES, nodes):
+                    piece = slice(first_node, first_node + nodes)
                     first_column = (t * NODES + first_node) // 16
-                    product = ring.tile([P, nodes], F32, name="product", tag=f"product{nodes}")
                     nc.vector.tensor_tensor(
-                        product[:],
+                        product[:, piece],
                         q_window[:].indirect(offsets[:, first_column : first_column + nodes // 16]),
-                        q_plain[:, first_node : first_node + nodes],
+                        q_plain[:, piece],
                         ALU.mult,
                     )
-                    product_bf = ring.tile([P, nodes], BF16, name="product_bf", tag=f"product_bf{nodes}")
-                    if t < NEIGHBOURS - 1:
-                        nc.scalar.copy(product_bf[:], product[:])
+                    if first_column + nodes // 16 < LIST // 16:
+                        nc.scalar.copy(product_bf[:, piece], product[:, piece])
                     else:
-                        nc.scalar.copy(product_bf[:, 0:HALF], product[:, 0:HALF])
-                        nc.vector.tensor_copy(product_bf[:, HALF:NODES], product[:, HALF:NODES])
-                    sum_over_clusters(nc, co, product_bf[:], ones, first_node)
+                        nc.vector.tensor_copy(product_bf[:, piece], product[:, piece])
+                co = pairs.tile([P, RUN], F32, name="co")
+                sum_over_clusters(nc, co, product_bf, ones)
                 nc.scalar.activation(out=terms[:, t * RUN : (t + 1) * RUN], in_=co[:], func=ACT.Ln, scale=2.0**LN_SHIFT)
 
             result = held.tile([P, RUN], F32, name="result")

@@ -120,9 +120,10 @@ def tile_spatialselectivemrf_kernel(tc, z, offs, out):
             for t in range(NEIGHBOURS):
                 product = ring.tile([P, NODES], F32, name="product")
                 product_bf = ring.tile([P, NODES], BF16, name="product_bf")
-                nodes = HALF if t in (0, NEIGHBOURS - 1) else NODES
-                for first_node in range(0, NODES, nodes):
-                    piece = slice(first_node, first_node + nodes)
+                cuts = {0: [0, HALF, NODES], NEIGHBOURS - 1: [0, NODES - QUARTER, NODES]}.get(t, [0, NODES])
+                for first_node, end_node in zip(cuts[:-1], cuts[1:]):
+                    nodes = end_node - first_node
+                    piece = slice(first_node, end_node)
                     first_column = (t * NODES + first_node) // 16
                     nc.vector.tensor_tensor(
                         product[:, piece],

@@ -98,15 +98,24 @@ def tile_spatialselectivemrf_kernel(tc, z, offs, out):
                     nc.tensor.transpose(q_ps[g][:, b * P : (b + 1) * P], q_t[:, block * P : (block + 1) * P], identity[:])
                 nc.scalar.copy(q_window[:, quarter], q_ps[g][:])
 
-        with tc.psum_pool(name="pairs", bufs=2) as pairs, tc.psum_pool(name="total", bufs=1) as total:
-            score_ps = total.tile([P, RUN], F32, name="score_ps")
+            q_z_t = held.tile([P, NODES], F32, name="q_z_t")
             q_z = held.tile([P, NODES], BF16, name="q_z")
             for g in range(QUARTERS):
                 quarter = slice(g * QUARTER, (g + 1) * QUARTER)
-                nc.vector.tensor_tensor(q_z[:, quarter], q_window[:, quarter], z_sb[:, quarter], ALU.mult)
-                if (g + 1) * QUARTER == HALF:
-                    nc.vector.tensor_copy(q_plain[:, 0:HALF], q_window[:, 0:HALF])
+                nc.vector.tensor_tensor(q_z_t[:, quarter], q_t[:, quarter], z_t[g][:], ALU.mult)
+            nc.vector.tensor_copy(q_plain[:, 0:HALF], q_window[:, 0:HALF])
             nc.scalar.copy(q_plain[:, HALF:NODES], q_window[:, HALF:NODES])
+            for g in range(QUARTERS):
+                quarter = slice(g * QUARTER, (g + 1) * QUARTER)
+                for b in range(QUARTER_BLOCKS):
+                    block = g * QUARTER_BLOCKS + b
+                    nc.tensor.transpose(
+                        q_ps[(g + 2) % QUARTERS][:, b * P : (b + 1) * P], q_z_t[:, block * P : (block + 1) * P], identity[:]
+                    )
+                nc.scalar.copy(q_z[:, quarter], q_ps[(g + 2) % QUARTERS][:])
+
+        with tc.psum_pool(name="pairs", bufs=2) as pairs, tc.psum_pool(name="total", bufs=1) as total:
+            score_ps = total.tile([P, RUN], F32, name="score_ps")
             sum_over_clusters(nc, score_ps, q_z, ones)
 
             terms = held.tile([P, (NEIGHBOURS + 1) * RUN], F32, name="terms")

@@ -95,8 +95,13 @@ def tile_spatialselectivemrf_kernel(tc, z, offs, out):
                         scalar2=None,
                         op0=ALU.mult,
                     )
-                    nc.tensor.transpose(q_ps[g][:, b * P : (b + 1) * P], q_t[:, block * P : (block + 1) * P], identity[:])
-                nc.scalar.copy(q_window[:, quarter], q_ps[g][:])
+                    if block < BLOCKS - 1:
+                        nc.tensor.transpose(q_ps[g][:, b * P : (b + 1) * P], q_t[:, block * P : (block + 1) * P], identity[:])
+                if g < QUARTERS - 1:
+                    nc.scalar.copy(q_window[:, quarter], q_ps[g][:])
+            nc.tensor.transpose(q_ps[0][:, 0:P], q_t[:, NODES - P : NODES], identity[:])
+            nc.scalar.copy(q_window[:, NODES - 2 * P : NODES - P], q_ps[QUARTERS - 1][:, 0:P])
+            nc.scalar.copy(q_window[:, NODES - P : NODES], q_ps[0][:, 0:P])
 
             q_z_t = held.tile([P, NODES], F32, name="q_z_t")
             q_z = held.tile([P, NODES], BF16, name="q_z")

@@ -123,9 +123,11 @@ def tile_spatialselectivemrf_kernel(tc, z, offs, out):
             score_ps = total.tile([P, RUN], F32, name="score_ps")
             sum_over_clusters(nc, score_ps, q_z, ones)
 
-            terms = held.tile([P, (NEIGHBOURS + 1) * RUN], F32, name="terms")
+            last = NEIGHBOURS - 1
+            terms = held.tile([P, NEIGHBOURS * RUN], F32, name="terms")
+            last_logs = held.tile([P, RUN], F32, name="last_logs")
             nc.scalar.activation(
-                out=terms[:, NEIGHBOURS * RUN : (NEIGHBOURS + 1) * RUN],
+                out=terms[:, last * RUN : (last + 1) * RUN],
                 in_=score_ps[:],
                 func=ACT.Copy,
                 bias=-NEIGHBOURS * LN_SHIFT * math.log(2.0),
@@ -134,7 +136,7 @@ def tile_spatialselectivemrf_kernel(tc, z, offs, out):
             for t in range(NEIGHBOURS):
                 product = ring.tile([P, NODES], F32, name="product")
                 product_bf = ring.tile([P, NODES], BF16, name="product_bf")
-                cuts = {0: [0, HALF, NODES], NEIGHBOURS - 1: [0, NODES - QUARTER, NODES]}.get(t, [0, NODES])
+                cuts = {0: [0, HALF, NODES], last: [0, NODES - QUARTER, NODES]}.get(t, [0, NODES])
                 for first_node, end_node in zip(cuts[:-1], cuts[1:]):
                     nodes = end_node - first_node
                     piece = slice(first_node, end_node)
@@ -151,14 +153,17 @@ def tile_spatialselectivemrf_kernel(tc, z, offs, out):
                         nc.vector.tensor_copy(product_bf[:, piece], product[:, piece])
                 co = pairs.tile([P, RUN], F32, name="co")
                 sum_over_clusters(nc, co, product_bf, ones)
-                nc.scalar.activation(out=terms[:, t * RUN : (t + 1) * RUN], in_=co[:], func=ACT.Ln, scale=2.0**LN_SHIFT)
+                logs = terms[:, t * RUN : (t + 1) * RUN] if t < last else last_logs[:]
+                nc.scalar.activation(out=logs, in_=co[:], func=ACT.Ln, scale=2.0**LN_SHIFT)
 
+            negative_sum = held.tile([P, RUN], F32, name="negative_sum")
             result = held.tile([P, RUN], F32, name="result")
             nc.vector.tensor_reduce(
-                out=result[:],
+                out=negative_sum[:],
                 in_=terms[:].rearrange("p (t r) -> p r t", r=RUN),
                 axis=mybir.AxisListType.X,
                 op=ALU.add,
                 negate=True,
             )
+            nc.vector.tensor_tensor(result[:], negative_sum[:], last_logs[:], ALU.subtract)
             nc.sync.dma_start(out.rearrange("o (p r) -> (o p) r", r=RUN), result[:])

import math

import concourse.mybir as mybir
from concourse.masks import make_identity

F32 = mybir.dt.float32
BF16 = mybir.dt.bfloat16
U16 = mybir.dt.uint16
ALU = mybir.AluOpType
ACT = mybir.ActivationFunctionType

P = 128
NODES = 1024
NEIGHBOURS = 6
LIST = NEIGHBOURS * NODES
BLOCKS = NODES // P
QUARTER = 256
QUARTERS = NODES // QUARTER
QUARTER_BLOCKS = QUARTER // P
HALF = NODES // 2
RUN = 8

LN_SHIFT = 62

FLOPS = 2 * P * (LIST + 2 * NODES)


def sum_over_clusters(nc, sums, products, ones):
    by_run = products[:].rearrange("c (p r) -> c r p", r=RUN)
    for r in range(RUN):
        nc.tensor.matmul(sums[:, r : r + 1], lhsT=by_run[:, r, :], rhs=ones[:], start=True, stop=True)


def tile_spatialselectivemrf_kernel(tc, z, offs, out):
    nc = tc.nc
    with tc.tile_pool(name="held", bufs=1) as held, tc.tile_pool(name="ring", bufs=3) as ring:
        z_sb = held.tile([P, NODES], F32, name="z_sb")
        offsets = held.tile([P, LIST // 16], U16, name="offsets")
        for g in range(QUARTERS):
            quarter = slice(g * QUARTER, (g + 1) * QUARTER)
            nc.sync.dma_start(z_sb[:, quarter], z[:, quarter])
        nc.sync.dma_start(offsets[:], offs)

        identity = held.tile([P, P], F32, name="identity")
        make_identity(nc, identity[:])
        ones = held.tile([P, 1], BF16, name="ones")
        nc.vector.memset(ones[:], 1.0)

        neg_max = held.tile([P, BLOCKS], F32, name="neg_max")
        exp_sum = held.tile([P, BLOCKS], F32, name="exp_sum")
        inv_sum = held.tile([P, BLOCKS], F32, name="inv_sum")
        e_t = held.tile([P, NODES], F32, name="e_t")
        q_t = held.tile([P, NODES], F32, name="q_t")
        q_window = held.tile([P, NODES], F32, name="q_window")
        q_plain = held.tile([P, NODES], F32, name="q_plain")

        with tc.psum_pool(name="flipped", bufs=1) as flipped:
            z_t = [flipped.tile([P, QUARTER], F32, name=f"z_t{g}") for g in range(QUARTERS)]
            q_ps = [flipped.tile([P, QUARTER], F32, name=f"q_ps{g}") for g in range(QUARTERS)]

            for g in range(QUARTERS):
                stats = slice(g * QUARTER_BLOCKS, (g + 1) * QUARTER_BLOCKS)
                for b in range(QUARTER_BLOCKS):
                    block = g * QUARTER_BLOCKS + b
                    nc.tensor.transpose(z_t[g][:, b * P : (b + 1) * P], z_sb[:, block * P : (block + 1) * P], identity[:])
                nc.vector.tensor_reduce(
                    out=neg_max[:, stats],
                    in_=z_t[g][:].rearrange("p (b c) -> p b c", c=P),
                    axis=mybir.AxisListType.X,
                    op=ALU.max,
                    negate=True,
                )
                for b in range(QUARTER_BLOCKS):
                    block = g * QUARTER_BLOCKS + b
                    nc.scalar.activation(
                        out=e_t[:, block * P : (block + 1) * P],
                        in_=z_t[g][:, b * P : (b + 1) * P],
                        func=ACT.Exp,
                        bias=neg_max[:, block : block + 1],
                        scale=1.0,
                        accum_out=exp_sum[:, block : block + 1],
                    )

            for g in range(QUARTERS):
                quarter = slice(g * QUARTER, (g + 1) * QUARTER)
                if g % 2 == 0:
                    stats = slice(g * QUARTER_BLOCKS, (g + 2) * QUARTER_BLOCKS)
                    nc.vector.reciprocal(inv_sum[:, stats], exp_sum[:, stats])
                for b in range(QUARTER_BLOCKS):
                    block = g * QUARTER_BLOCKS + b
                    nc.vector.tensor_scalar(
                        out=q_t[:, block * P : (block + 1) * P],
                        in0=e_t[:, block * P : (block + 1) * P],
                        scalar1=inv_sum[:, block : block + 1],
                        scalar2=None,
                        op0=ALU.mult,
                    )
                    if block < BLOCKS - 1:
                        nc.tensor.transpose(q_ps[g][:, b * P : (b + 1) * P], q_t[:, block * P : (block + 1) * P], identity[:])
                if g < QUARTERS - 1:
                    nc.scalar.copy(q_window[:, quarter], q_ps[g][:])
            nc.tensor.transpose(q_ps[0][:, 0:P], q_t[:, NODES - P : NODES], identity[:])
            nc.scalar.copy(q_window[:, NODES - 2 * P : NODES - P], q_ps[QUARTERS - 1][:, 0:P])
            nc.scalar.copy(q_window[:, NODES - P : NODES], q_ps[0][:, 0:P])

            q_z_t = held.tile([P, NODES], F32, name="q_z_t")
            q_z = held.tile([P, NODES], BF16, name="q_z")
            for g in range(QUARTERS):
                quarter = slice(g * QUARTER, (g + 1) * QUARTER)
                nc.vector.tensor_tensor(q_z_t[:, quarter], q_t[:, quarter], z_t[g][:], ALU.mult)
            nc.vector.tensor_copy(q_plain[:, 0:HALF], q_window[:, 0:HALF])
            nc.scalar.copy(q_plain[:, HALF:NODES], q_window[:, HALF:NODES])
            for g in range(QUARTERS):
                quarter = slice(g * QUARTER, (g + 1) * QUARTER)
                for b in range(QUARTER_BLOCKS):
                    block = g * QUARTER_BLOCKS + b
                    nc.tensor.transpose(
                        q_ps[(g + 2) % QUARTERS][:, b * P : (b + 1) * P], q_z_t[:, block * P : (block + 1) * P], identity[:]
                    )
                nc.scalar.copy(q_z[:, quarter], q_ps[(g + 2) % QUARTERS][:])

        with tc.psum_pool(name="pairs", bufs=2) as pairs, tc.psum_pool(name="total", bufs=1) as total:
            score_ps = total.tile([P, RUN], F32, name="score_ps")
            sum_over_clusters(nc, score_ps, q_z, ones)

            last = NEIGHBOURS - 1
            terms = held.tile([P, NEIGHBOURS * RUN], F32, name="terms")
            last_logs = held.tile([P, RUN], F32, name="last_logs")
            nc.scalar.activation(
                out=terms[:, last * RUN : (last + 1) * RUN],
                in_=score_ps[:],
                func=ACT.Copy,
                bias=-NEIGHBOURS * LN_SHIFT * math.log(2.0),
            )

            for t in range(NEIGHBOURS):
                product = ring.tile([P, NODES], F32, name="product")
                product_bf = ring.tile([P, NODES], BF16, name="product_bf")
                cuts = {0: [0, HALF, NODES], last: [0, NODES - QUARTER, NODES]}.get(t, [0, NODES])
                for first_node, end_node in zip(cuts[:-1], cuts[1:]):
                    nodes = end_node - first_node
                    piece = slice(first_node, end_node)
                    first_column = (t * NODES + first_node) // 16
                    nc.vector.tensor_tensor(
                        product[:, piece],
                        q_window[:].indirect(offsets[:, first_column : first_column + nodes // 16]),
                        q_plain[:, piece],
                        ALU.mult,
                    )
                    if first_column + nodes // 16 < LIST // 16:
                        nc.scalar.copy(product_bf[:, piece], product[:, piece])
                    else:
                        nc.vector.tensor_copy(product_bf[:, piece], product[:, piece])
                co = pairs.tile([P, RUN], F32, name="co")
                sum_over_clusters(nc, co, product_bf, ones)
                logs = terms[:, t * RUN : (t + 1) * RUN] if t < last else last_logs[:]
                nc.scalar.activation(out=logs, in_=co[:], func=ACT.Ln, scale=2.0**LN_SHIFT)

            negative_sum = held.tile([P, RUN], F32, name="negative_sum")
            result = held.tile([P, RUN], F32, name="result")
            nc.vector.tensor_reduce(
                out=negative_sum[:],
                in_=terms[:].rearrange("p (t r) -> p r t", r=RUN),
                axis=mybir.AxisListType.X,
                op=ALU.add,
                negate=True,
            )
            nc.vector.tensor_tensor(result[:], negative_sum[:], last_logs[:], ALU.subtract)
            nc.sync.dma_start(out.rearrange("o (p r) -> (o p) r", r=RUN), result[:])
